import numpy as np
import ml_dtypes


def mxq(x, axis, fmt="e4m3"):
    dtype, down = {"e4m3": (ml_dtypes.float8_e4m3fn, 7), "e5m2": (ml_dtypes.float8_e5m2, 14)}[fmt]
    v = np.moveaxis(np.asarray(x, np.float32).astype(ml_dtypes.bfloat16).astype(np.float64), axis, -1)
    blocks = v.reshape(v.shape[:-1] + (-1, 32))
    amax = np.abs(blocks).max(-1, keepdims=True)
    byte = np.maximum(np.where(amax > 0, np.frexp(amax)[1] - 1 + 127, 0) - down, 1)
    scale = np.exp2(byte - 127.0)
    codes = (blocks / scale).astype(np.float32).astype(dtype).astype(np.float64)
    return np.moveaxis((codes * scale).reshape(v.shape), -1, axis)


WIDE = False


def mx_kscale(k):
    if not WIDE:
        return np.ones(k)
    levels = np.array([10, -10, 5, -5, 0])
    a = np.random.permutation(np.resize(levels, k // 512 * 4)).reshape(k // 512, 4)
    idx = np.arange(k)
    return np.exp2(a[idx // 512, idx % 128 // 32])


BF16 = ml_dtypes.bfloat16


def bf(x):
    return np.asarray(x, np.float32).astype(BF16)


def f64(x):
    return np.asarray(x).astype(np.float64)


B, T, S, H, C, CO, W = 2, 128, 16, 8, 1024, 1024, 5
HD = C // H


def setup_inputs():
    t = mx_kscale(C)
    i = np.arange(T)
    band = np.abs(i[:, None] - i[None, :]) <= W
    e = np.exp(np.random.standard_normal((B, H, S, T, T))) * band
    return {"attn": bf(e / e.sum(-1, keepdims=True)),
            "v": bf(np.random.standard_normal((B, T, S, H, HD)) * t.reshape(H, HD)),
            "W_out": bf(np.random.standard_normal((C, CO)) / np.sqrt(C) / t[:, None])}


def reference(attn, v, W_out):
    ctx = f64(attn) @ f64(v).transpose(0, 3, 2, 1, 4)
    ctx = ctx.transpose(0, 3, 2, 1, 4).reshape(B * T * S, C)
    return (mxq(ctx, 1, "e4m3") @ mxq(f64(W_out), 0, "e4m3")).reshape(B, T * S, CO)

@@ -1,0 +1,180 @@
+from contextlib import ExitStack
+
+import concourse.masks as masks
+import concourse.mybir as mybir
+
+BF16 = mybir.dt.bfloat16
+F32 = mybir.dt.float32
+U32 = mybir.dt.uint32
+U8 = mybir.dt.uint8
+FP8X4 = mybir.dt.float8_e4m3fn_x4
+
+P = 128
+B, S, H, CO = 2, 16, 8, 1024
+PACK = 4
+PASSES = H // PACK
+N_HALF = 512
+FRAMES_PER_ROW = 8
+ROWS_PER_MATRIX = P // FRAMES_PER_ROW
+S_GROUP = P // ROWS_PER_MATRIX
+S_LOAD = 4
+GROUPS = B * S // S_GROUP
+STEPS = B * S
+LAG = 2
+
+FLOPS = 2 * B * H * S * P * P * P + 2 * B * S * P * H * P * CO
+
+
+def tile_localtemporalattention_pa_kernel(tc, attn, v, W_out, out):
+    nc = tc.nc
+    with ExitStack() as stack:
+        stack.enter_context(tc.manual_schedule())
+        const = stack.enter_context(tc.tile_pool(name="const", bufs=1))
+        attn_pool = stack.enter_context(tc.tile_pool(name="attn", bufs=6))
+        v_pool = stack.enter_context(tc.tile_pool(name="v", bufs=6))
+        flipped_pool = stack.enter_context(tc.tile_pool(name="flipped", bufs=2 * H))
+        ctx_pool = stack.enter_context(tc.tile_pool(name="ctx", bufs=3))
+        code_pool = stack.enter_context(tc.tile_pool(name="codes", bufs=4))
+        out_pool = stack.enter_context(tc.tile_pool(name="out", bufs=6))
+        psum = stack.enter_context(tc.psum_pool(name="psum", bufs=8))
+
+        attn_rows = {}
+        v_rows = {}
+        attn_t = {}
+        ctx_bf16 = {}
+        ctx_codes = {}
+        ctx_scales = {}
+
+        def load_attn(group, g):
+            b, s_half = divmod(group, S // S_GROUP)
+            rows = attn_pool.tile([P, PACK, FRAMES_PER_ROW * P], BF16, name="attn_rows")
+            nc.sync.dma_start(
+                out=rows[:],
+                in_=attn[
+                    b, PACK * g : PACK * (g + 1), S_GROUP * s_half : S_GROUP * (s_half + 1)
+                ].rearrange("hh s (th j) u -> (s th) hh (j u)", j=FRAMES_PER_ROW),
+            )
+            attn_rows[(group, g)] = rows
+
+        def load_v(group, half):
+            b, s_half = divmod(group, S // S_GROUP)
+            s0 = S_GROUP * s_half + S_LOAD * half
+            rows = v_pool.tile([P, S_LOAD, H, P], BF16, name="v_rows")
+            nc.sync.dma_start(out=rows[:], in_=v[b, :, s0 : s0 + S_LOAD])
+            v_rows[(group, half)] = rows
+
+        def load_round(group):
+            for half in range(PASSES):
+                load_v(group, half)
+                if group + 1 < GROUPS:
+                    load_attn(group + 1, half)
+
+        def transpose_head(group, h, copy):
+            rows = attn_rows[(group, h // PACK)]
+            bank = psum.tile([P, FRAMES_PER_ROW, P], BF16, name="flip_bank", tag="bank")
+            for j in range(FRAMES_PER_ROW):
+                nc.tensor.transpose(bank[:, j, :], rows[:, h % PACK, P * j : P * (j + 1)], ident[:])
+            flipped = flipped_pool.tile([P, S_GROUP, P], BF16, name="flipped")
+            copy(
+                out=flipped[:].rearrange("u s (j th) -> u s j th", j=FRAMES_PER_ROW),
+                in_=bank[:].rearrange("u j (s th) -> u s j th", s=S_GROUP),
+            )
+            attn_t[(group, h)] = flipped
+
+        def mix_frames(step, g):
+            group, s_local = divmod(step, S_GROUP)
+            values = v_rows[(group, s_local // S_LOAD)]
+            bank = psum.tile([P, PACK, P], F32, name="ctx_bank", tag="bank")
+            for hh in range(PACK):
+                h = PACK * g + hh
+                nc.tensor.matmul(
+                    out=bank[:, hh, :],
+                    lhsT=values[:, s_local % S_LOAD, h, :],
+                    rhs=attn_t[(group, h)][:, s_local, :],
+                    start=True,
+                    stop=True,
+                )
+            nc.scalar.copy(
+                out=ctx_bf16[step][:, g].rearrange("d (th j) hh -> d th j hh", j=FRAMES_PER_ROW),
+                in_=bank[:].rearrange("d hh (j th) -> d th j hh", j=FRAMES_PER_ROW),
+            )
+
+        def quantise_ctx(step):
+            codes = code_pool.tile([P, PASSES * P], U32, name="ctx_codes", align_bytes=64)
+            scales = code_pool.tile([P, PASSES * P], U8, name="ctx_scales", align_bytes=64)
+            nc.vector.quantize_mx(
+                out=codes[:].bitcast(FP8X4),
+                scales=scales[:],
+                in_=ctx_bf16[step][:].rearrange("d g t hh -> d (g t hh)"),
+            )
+            ctx_codes[step] = codes
+            ctx_scales[step] = scales
+
+        def project(step):
+            b, s = divmod(step, S)
+            result = out_pool.tile([P, CO], F32, name="result")
+            for half, copy in enumerate((nc.scalar.copy, nc.vector.tensor_copy)):
+                cols = slice(N_HALF * half, N_HALF * (half + 1))
+                bank = psum.tile([P, N_HALF], F32, name="out_bank", tag="bank")
+                for g in range(PASSES):
+                    rows = slice(P * g, P * (g + 1))
+                    nc.tensor.matmul_mx(
+                        out=bank[:],
+                        lhsT=ctx_codes[step][:, rows].bitcast(FP8X4),
+                        lhsT_scale=ctx_scales[step][:, rows],
+                        rhs=w_codes[:, g, cols].bitcast(FP8X4),
+                        rhs_scale=w_scales[:, g, cols],
+                        start=(g == 0),
+                        stop=(g == PASSES - 1),
+                    )
+                copy(out=result[:, cols], in_=bank[:])
+            nc.gpsimd.dma_start(
+                out=out[b].rearrange("(t s) c -> s t c", s=S)[s], in_=result[:]
+            )
+
+        w_raw = []
+        for g in range(PASSES):
+            load_attn(0, g)
+            raw = const.tile([P, PACK, CO], BF16, name="w_raw%d" % g)
+            nc.sync.dma_start(
+                out=raw[:],
+                in_=W_out[PACK * P * g : PACK * P * (g + 1), :].rearrange("(hh d) n -> d hh n", d=P),
+            )
+            w_raw.append(raw)
+        load_round(0)
+        load_round(1)
+
+        ident = const.tile([P, P], BF16, name="ident")
+        masks.make_identity(nc, ident[:])
+
+        w_codes = const.tile([P, PASSES, CO], U32, name="w_codes", align_bytes=64)
+        w_scales = const.tile([P, PASSES, CO], U8, name="w_scales", align_bytes=64)
+        w_grouped = []
+        for g in range(PASSES):
+            grouped = const.tile([P, CO, PACK], BF16, name="w_grouped%d" % g, align_bytes=64)
+            nc.vector.tensor_copy(out=grouped[:], in_=w_raw[g][:].rearrange("d hh n -> d n hh"))
+            w_grouped.append(grouped)
+        for g in range(PASSES):
+            nc.vector.quantize_mx(
+                out=w_codes[:, g, :].bitcast(FP8X4),
+                scales=w_scales[:, g, :],
+                in_=w_grouped[g][:].rearrange("d n hh -> d (n hh)"),
+            )
+
+        for h in range(H):
+            transpose_head(0, h, nc.scalar.copy)
+
+        for step in range(STEPS + LAG):
+            if step < STEPS:
+                group, s_local = divmod(step, S_GROUP)
+                if s_local == 0 and group + 2 < GROUPS:
+                    load_round(group + 2)
+                ctx_bf16[step] = ctx_pool.tile([P, PASSES, P, PACK], BF16, name="ctx_bf16", align_bytes=64)
+                mix_frames(step, 0)
+                if group + 1 < GROUPS:
+                    transpose_head(group + 1, s_local, nc.vector.tensor_copy)
+                mix_frames(step, 1)
+            if 1 <= step <= STEPS:
+                quantise_ctx(step - 1)
+            if step >= LAG:
+                project(step - LAG)

@@ -13,14 +13,16 @@ P = 128
 B, S, H, CO = 2, 16, 8, 1024
 PACK = 4
 PASSES = H // PACK
-N_HALF = 512
-FRAMES_PER_ROW = 8
-ROWS_PER_MATRIX = P // FRAMES_PER_ROW
-S_GROUP = P // ROWS_PER_MATRIX
-S_LOAD = 4
+BANK_COLS = 512
+COL_HALVES = CO // BANK_COLS
+J = 8
+TH = P // J
+S_GROUP = P // TH
 GROUPS = B * S // S_GROUP
+S_PAIR = 2
 STEPS = B * S
 LAG = 2
+AHEAD = 8
 
 FLOPS = 2 * B * H * S * P * P * P + 2 * B * S * P * H * P * CO
 
@@ -30,82 +32,98 @@ def tile_localtemporalattention_pa_kernel(tc, attn, v, W_out, out):
     with ExitStack() as stack:
         stack.enter_context(tc.manual_schedule())
         const = stack.enter_context(tc.tile_pool(name="const", bufs=1))
-        attn_pool = stack.enter_context(tc.tile_pool(name="attn", bufs=6))
-        v_pool = stack.enter_context(tc.tile_pool(name="v", bufs=6))
+        attn_pool = stack.enter_context(tc.tile_pool(name="attn", bufs=AHEAD + 4))
+        v_pool = stack.enter_context(tc.tile_pool(name="v", bufs=AHEAD // S_PAIR + 2))
         flipped_pool = stack.enter_context(tc.tile_pool(name="flipped", bufs=2 * H))
         ctx_pool = stack.enter_context(tc.tile_pool(name="ctx", bufs=3))
-        code_pool = stack.enter_context(tc.tile_pool(name="codes", bufs=4))
+        code_pool = stack.enter_context(tc.tile_pool(name="codes", bufs=LAG + 2))
         out_pool = stack.enter_context(tc.tile_pool(name="out", bufs=6))
         psum = stack.enter_context(tc.psum_pool(name="psum", bufs=8))
 
         attn_rows = {}
         v_rows = {}
         attn_t = {}
-        ctx_bf16 = {}
         ctx_codes = {}
         ctx_scales = {}
 
-        def load_attn(group, g):
+        def load_attn(group, h):
             b, s_half = divmod(group, S // S_GROUP)
-            rows = attn_pool.tile([P, PACK, FRAMES_PER_ROW * P], BF16, name="attn_rows")
+            rows = attn_pool.tile([P, J * P], BF16, name="attn_rows")
             nc.sync.dma_start(
                 out=rows[:],
-                in_=attn[
-                    b, PACK * g : PACK * (g + 1), S_GROUP * s_half : S_GROUP * (s_half + 1)
-                ].rearrange("hh s (th j) u -> (s th) hh (j u)", j=FRAMES_PER_ROW),
+                in_=attn[b, h, S_GROUP * s_half : S_GROUP * (s_half + 1)].rearrange(
+                    "s (th j) u -> (s th) (j u)", j=J
+                ),
             )
-            attn_rows[(group, g)] = rows
+            attn_rows[(group, h)] = rows
 
-        def load_v(group, half):
-            b, s_half = divmod(group, S // S_GROUP)
-            s0 = S_GROUP * s_half + S_LOAD * half
-            rows = v_pool.tile([P, S_LOAD, H, P], BF16, name="v_rows")
-            nc.sync.dma_start(out=rows[:], in_=v[b, :, s0 : s0 + S_LOAD])
-            v_rows[(group, half)] = rows
+        def load_for(step):
+            if step >= STEPS:
+                return
+            if step % S_PAIR == 0:
+                b, s = divmod(step, S)
+                rows = v_pool.tile([P, S_PAIR, H, P], BF16, name="v_rows")
+                nc.sync.dma_start(out=rows[:], in_=v[b, :, s : s + S_PAIR])
+                v_rows[step // S_PAIR] = rows
+            group, h = divmod(step, S_GROUP)
+            if group + 1 < GROUPS:
+                load_attn(group + 1, h)
 
-        def load_round(group):
-            for half in range(PASSES):
-                load_v(group, half)
-                if group + 1 < GROUPS:
-                    load_attn(group + 1, half)
+        def transpose_slice(bank, group, h, j):
+            nc.tensor.transpose(bank[:, j, :], attn_rows[(group, h)][:, P * j : P * (j + 1)], ident[:])
 
-        def transpose_head(group, h, copy):
-            rows = attn_rows[(group, h // PACK)]
-            bank = psum.tile([P, FRAMES_PER_ROW, P], BF16, name="flip_bank", tag="bank")
-            for j in range(FRAMES_PER_ROW):
-                nc.tensor.transpose(bank[:, j, :], rows[:, h % PACK, P * j : P * (j + 1)], ident[:])
+        def keep_flipped(bank, group, h, copy):
             flipped = flipped_pool.tile([P, S_GROUP, P], BF16, name="flipped")
             copy(
-                out=flipped[:].rearrange("u s (j th) -> u s j th", j=FRAMES_PER_ROW),
+                out=flipped[:].rearrange("u s (j th) -> u s j th", j=J),
                 in_=bank[:].rearrange("u j (s th) -> u s j th", s=S_GROUP),
             )
             attn_t[(group, h)] = flipped
 
-        def mix_frames(step, g):
+        def mix_and_transpose(step):
             group, s_local = divmod(step, S_GROUP)
-            values = v_rows[(group, s_local // S_LOAD)]
-            bank = psum.tile([P, PACK, P], F32, name="ctx_bank", tag="bank")
-            for hh in range(PACK):
-                h = PACK * g + hh
+            values = v_rows[step // S_PAIR]
+            ctx_bf16 = ctx_pool.tile([P, PASSES, P, PACK], BF16, name="ctx_bf16", align_bytes=64)
+            ctx_banks = [
+                psum.tile([P, PACK, P], F32, name="ctx_bank%d" % g, tag="bank") for g in range(PASSES)
+            ]
+            more = group + 1 < GROUPS
+            if more:
+                flip_bank = psum.tile([P, J, P], BF16, name="flip_bank", tag="bank")
+
+            def mix(h):
+                g, hh = divmod(h, PACK)
                 nc.tensor.matmul(
-                    out=bank[:, hh, :],
-                    lhsT=values[:, s_local % S_LOAD, h, :],
+                    out=ctx_banks[g][:, hh, :],
+                    lhsT=values[:, step % S_PAIR, h, :],
                     rhs=attn_t[(group, h)][:, s_local, :],
                     start=True,
                     stop=True,
                 )
-            nc.scalar.copy(
-                out=ctx_bf16[step][:, g].rearrange("d (th j) hh -> d th j hh", j=FRAMES_PER_ROW),
-                in_=bank[:].rearrange("d hh (j th) -> d th j hh", j=FRAMES_PER_ROW),
-            )
 
-        def quantise_ctx(step):
+            for pair in range(H // 2):
+                mix(2 * pair)
+                if more:
+                    transpose_slice(flip_bank, group + 1, s_local, 2 * pair)
+                    transpose_slice(flip_bank, group + 1, s_local, 2 * pair + 1)
+                mix(2 * pair + 1)
+                if (2 * pair + 2) % PACK == 0:
+                    g = (2 * pair + 1) // PACK
+                    nc.scalar.copy(
+                        out=ctx_bf16[:, g].rearrange("d (th j) hh -> d th j hh", j=J),
+                        in_=ctx_banks[g][:].rearrange("d hh (j th) -> d th j hh", j=J),
+                    )
+            if more:
+                keep_flipped(flip_bank, group + 1, s_local, nc.vector.tensor_copy)
+            return ctx_bf16
+
+        def quantise_ctx(step, ctx_bf16):
             codes = code_pool.tile([P, PASSES * P], U32, name="ctx_codes", align_bytes=64)
             scales = code_pool.tile([P, PASSES * P], U8, name="ctx_scales", align_bytes=64)
             nc.vector.quantize_mx(
                 out=codes[:].bitcast(FP8X4),
                 scales=scales[:],
-                in_=ctx_bf16[step][:].rearrange("d g t hh -> d (g t hh)"),
+                in_=ctx_bf16[:].rearrange("d g t hh -> d (g t hh)"),
             )
             ctx_codes[step] = codes
             ctx_scales[step] = scales
@@ -114,8 +132,8 @@ def tile_localtemporalattention_pa_kernel(tc, attn, v, W_out, out):
             b, s = divmod(step, S)
             result = out_pool.tile([P, CO], F32, name="result")
             for half, copy in enumerate((nc.scalar.copy, nc.vector.tensor_copy)):
-                cols = slice(N_HALF * half, N_HALF * (half + 1))
-                bank = psum.tile([P, N_HALF], F32, name="out_bank", tag="bank")
+                cols = slice(BANK_COLS * half, BANK_COLS * (half + 1))
+                bank = psum.tile([P, BANK_COLS], F32, name="out_bank", tag="bank")
                 for g in range(PASSES):
                     rows = slice(P * g, P * (g + 1))
                     nc.tensor.matmul_mx(
@@ -128,53 +146,55 @@ def tile_localtemporalattention_pa_kernel(tc, attn, v, W_out, out):
                         stop=(g == PASSES - 1),
                     )
                 copy(out=result[:, cols], in_=bank[:])
-            nc.gpsimd.dma_start(
-                out=out[b].rearrange("(t s) c -> s t c", s=S)[s], in_=result[:]
-            )
+            nc.sync.dma_start(out=out[b].rearrange("(t s) c -> s t c", s=S)[s], in_=result[:])
 
         w_raw = []
         for g in range(PASSES):
-            load_attn(0, g)
+            for hh in range(PACK):
+                load_attn(0, PACK * g + hh)
             raw = const.tile([P, PACK, CO], BF16, name="w_raw%d" % g)
             nc.sync.dma_start(
                 out=raw[:],
                 in_=W_out[PACK * P * g : PACK * P * (g + 1), :].rearrange("(hh d) n -> d hh n", d=P),
             )
             w_raw.append(raw)
-        load_round(0)
-        load_round(1)
 
         ident = const.tile([P, P], BF16, name="ident")
         masks.make_identity(nc, ident[:])
 
         w_codes = const.tile([P, PASSES, CO], U32, name="w_codes", align_bytes=64)
         w_scales = const.tile([P, PASSES, CO], U8, name="w_scales", align_bytes=64)
-        w_grouped = []
         for g in range(PASSES):
             grouped = const.tile([P, CO, PACK], BF16, name="w_grouped%d" % g, align_bytes=64)
-            nc.vector.tensor_copy(out=grouped[:], in_=w_raw[g][:].rearrange("d hh n -> d n hh"))
-            w_grouped.append(grouped)
-        for g in range(PASSES):
-            nc.vector.quantize_mx(
-                out=w_codes[:, g, :].bitcast(FP8X4),
-                scales=w_scales[:, g, :],
-                in_=w_grouped[g][:].rearrange("d n hh -> d (n hh)"),
-            )
+            for half in range(COL_HALVES):
+                cols = slice(BANK_COLS * half, BANK_COLS * (half + 1))
+                nc.vector.tensor_copy(
+                    out=grouped[:, cols, :].rearrange("d (c i) hh -> d c hh i", i=4),
+                    in_=w_raw[g][:, :, cols].rearrange("d hh (c i) -> d c hh i", i=4),
+                )
+            for half in range(COL_HALVES):
+                cols = slice(BANK_COLS * half, BANK_COLS * (half + 1))
+                nc.vector.quantize_mx(
+                    out=w_codes[:, g, cols].bitcast(FP8X4),
+                    scales=w_scales[:, g, cols],
+                    in_=grouped[:, cols, :].rearrange("d n hh -> d (n hh)"),
+                )
 
         for h in range(H):
-            transpose_head(0, h, nc.scalar.copy)
+            first_bank = psum.tile([P, J, P], BF16, name="first_bank", tag="bank")
+            for j in range(J):
+                transpose_slice(first_bank, 0, h, j)
+            keep_flipped(first_bank, 0, h, nc.scalar.copy)
 
+        for step in range(AHEAD):
+            load_for(step)
+
+        mixed = {}
         for step in range(STEPS + LAG):
             if step < STEPS:
-                group, s_local = divmod(step, S_GROUP)
-                if s_local == 0 and group + 2 < GROUPS:
-                    load_round(group + 2)
-                ctx_bf16[step] = ctx_pool.tile([P, PASSES, P, PACK], BF16, name="ctx_bf16", align_bytes=64)
-                mix_frames(step, 0)
-                if group + 1 < GROUPS:
-                    transpose_head(group + 1, s_local, nc.vector.tensor_copy)
-                mix_frames(step, 1)
+                load_for(step + AHEAD)
+                mixed[step] = mix_and_transpose(step)
             if 1 <= step <= STEPS:
-                quantise_ctx(step - 1)
+                quantise_ctx(step - 1, mixed[step - 1])
             if step >= LAG:
                 project(step - LAG)

from contextlib import ExitStack

import concourse.masks as masks
import concourse.mybir as mybir

BF16 = mybir.dt.bfloat16
F32 = mybir.dt.float32
U32 = mybir.dt.uint32
U8 = mybir.dt.uint8
FP8X4 = mybir.dt.float8_e4m3fn_x4

P = 128
B, S, H, CO = 2, 16, 8, 1024
PACK = 4
PASSES = H // PACK
BANK_COLS = 512
COL_HALVES = CO // BANK_COLS
J = 8
TH = P // J
S_GROUP = P // TH
GROUPS = B * S // S_GROUP
S_PAIR = 2
STEPS = B * S
LAG = 2
AHEAD = 8

FLOPS = 2 * B * H * S * P * P * P + 2 * B * S * P * H * P * CO


def tile_localtemporalattention_pa_kernel(tc, attn, v, W_out, out):
    nc = tc.nc
    with ExitStack() as stack:
        stack.enter_context(tc.manual_schedule())
        const = stack.enter_context(tc.tile_pool(name="const", bufs=1))
        attn_pool = stack.enter_context(tc.tile_pool(name="attn", bufs=AHEAD + 4))
        v_pool = stack.enter_context(tc.tile_pool(name="v", bufs=AHEAD // S_PAIR + 2))
        flipped_pool = stack.enter_context(tc.tile_pool(name="flipped", bufs=2 * H))
        ctx_pool = stack.enter_context(tc.tile_pool(name="ctx", bufs=3))
        code_pool = stack.enter_context(tc.tile_pool(name="codes", bufs=LAG + 2))
        out_pool = stack.enter_context(tc.tile_pool(name="out", bufs=6))
        psum = stack.enter_context(tc.psum_pool(name="psum", bufs=8))

        attn_rows = {}
        v_rows = {}
        attn_t = {}
        ctx_codes = {}
        ctx_scales = {}

        def load_attn(group, h):
            b, s_half = divmod(group, S // S_GROUP)
            rows = attn_pool.tile([P, J * P], BF16, name="attn_rows")
            nc.sync.dma_start(
                out=rows[:],
                in_=attn[b, h, S_GROUP * s_half : S_GROUP * (s_half + 1)].rearrange(
                    "s (th j) u -> (s th) (j u)", j=J
                ),
            )
            attn_rows[(group, h)] = rows

        def load_for(step):
            if step >= STEPS:
                return
            if step % S_PAIR == 0:
                b, s = divmod(step, S)
                rows = v_pool.tile([P, S_PAIR, H, P], BF16, name="v_rows")
                nc.sync.dma_start(out=rows[:], in_=v[b, :, s : s + S_PAIR])
                v_rows[step // S_PAIR] = rows
            group, h = divmod(step, S_GROUP)
            if group + 1 < GROUPS:
                load_attn(group + 1, h)

        def transpose_slice(bank, group, h, j):
            nc.tensor.transpose(bank[:, j, :], attn_rows[(group, h)][:, P * j : P * (j + 1)], ident[:])

        def keep_flipped(bank, group, h, copy):
            flipped = flipped_pool.tile([P, S_GROUP, P], BF16, name="flipped")
            copy(
                out=flipped[:].rearrange("u s (j th) -> u s j th", j=J),
                in_=bank[:].rearrange("u j (s th) -> u s j th", s=S_GROUP),
            )
            attn_t[(group, h)] = flipped

        def mix_and_transpose(step):
            group, s_local = divmod(step, S_GROUP)
            values = v_rows[step // S_PAIR]
            ctx_bf16 = ctx_pool.tile([P, PASSES, P, PACK], BF16, name="ctx_bf16", align_bytes=64)
            ctx_banks = [
                psum.tile([P, PACK, P], F32, name="ctx_bank%d" % g, tag="bank") for g in range(PASSES)
            ]
            more = group + 1 < GROUPS
            if more:
                flip_bank = psum.tile([P, J, P], BF16, name="flip_bank", tag="bank")

            def mix(h):
                g, hh = divmod(h, PACK)
                nc.tensor.matmul(
                    out=ctx_banks[g][:, hh, :],
                    lhsT=values[:, step % S_PAIR, h, :],
                    rhs=attn_t[(group, h)][:, s_local, :],
                    start=True,
                    stop=True,
                )

            for pair in range(H // 2):
                mix(2 * pair)
                if more:
                    transpose_slice(flip_bank, group + 1, s_local, 2 * pair)
                    transpose_slice(flip_bank, group + 1, s_local, 2 * pair + 1)
                mix(2 * pair + 1)
                if (2 * pair + 2) % PACK == 0:
                    g = (2 * pair + 1) // PACK
                    nc.scalar.copy(
                        out=ctx_bf16[:, g].rearrange("d (th j) hh -> d th j hh", j=J),
                        in_=ctx_banks[g][:].rearrange("d hh (j th) -> d th j hh", j=J),
                    )
            if more:
                keep_flipped(flip_bank, group + 1, s_local, nc.vector.tensor_copy)
            return ctx_bf16

        def quantise_ctx(step, ctx_bf16):
            codes = code_pool.tile([P, PASSES * P], U32, name="ctx_codes", align_bytes=64)
            scales = code_pool.tile([P, PASSES * P], U8, name="ctx_scales", align_bytes=64)
            nc.vector.quantize_mx(
                out=codes[:].bitcast(FP8X4),
                scales=scales[:],
                in_=ctx_bf16[:].rearrange("d g t hh -> d (g t hh)"),
            )
            ctx_codes[step] = codes
            ctx_scales[step] = scales

        def project(step):
            b, s = divmod(step, S)
            result = out_pool.tile([P, CO], F32, name="result")
            for half, copy in enumerate((nc.scalar.copy, nc.vector.tensor_copy)):
                cols = slice(BANK_COLS * half, BANK_COLS * (half + 1))
                bank = psum.tile([P, BANK_COLS], F32, name="out_bank", tag="bank")
                for g in range(PASSES):
                    rows = slice(P * g, P * (g + 1))
                    nc.tensor.matmul_mx(
                        out=bank[:],
                        lhsT=ctx_codes[step][:, rows].bitcast(FP8X4),
                        lhsT_scale=ctx_scales[step][:, rows],
                        rhs=w_codes[:, g, cols].bitcast(FP8X4),
                        rhs_scale=w_scales[:, g, cols],
                        start=(g == 0),
                        stop=(g == PASSES - 1),
                    )
                copy(out=result[:, cols], in_=bank[:])
            nc.sync.dma_start(out=out[b].rearrange("(t s) c -> s t c", s=S)[s], in_=result[:])

        w_raw = []
        for g in range(PASSES):
            for hh in range(PACK):
                load_attn(0, PACK * g + hh)
            raw = const.tile([P, PACK, CO], BF16, name="w_raw%d" % g)
            nc.sync.dma_start(
                out=raw[:],
                in_=W_out[PACK * P * g : PACK * P * (g + 1), :].rearrange("(hh d) n -> d hh n", d=P),
            )
            w_raw.append(raw)

        ident = const.tile([P, P], BF16, name="ident")
        masks.make_identity(nc, ident[:])

        w_codes = const.tile([P, PASSES, CO], U32, name="w_codes", align_bytes=64)
        w_scales = const.tile([P, PASSES, CO], U8, name="w_scales", align_bytes=64)
        for g in range(PASSES):
            grouped = const.tile([P, CO, PACK], BF16, name="w_grouped%d" % g, align_bytes=64)
            for half in range(COL_HALVES):
                cols = slice(BANK_COLS * half, BANK_COLS * (half + 1))
                nc.vector.tensor_copy(
                    out=grouped[:, cols, :].rearrange("d (c i) hh -> d c hh i", i=4),
                    in_=w_raw[g][:, :, cols].rearrange("d hh (c i) -> d c hh i", i=4),
                )
            for half in range(COL_HALVES):
                cols = slice(BANK_COLS * half, BANK_COLS * (half + 1))
                nc.vector.quantize_mx(
                    out=w_codes[:, g, cols].bitcast(FP8X4),
                    scales=w_scales[:, g, cols],
                    in_=grouped[:, cols, :].rearrange("d n hh -> d (n hh)"),
                )

        for h in range(H):
            first_bank = psum.tile([P, J, P], BF16, name="first_bank", tag="bank")
            for j in range(J):
                transpose_slice(first_bank, 0, h, j)
            keep_flipped(first_bank, 0, h, nc.scalar.copy)

        for step in range(AHEAD):
            load_for(step)

        mixed = {}
        for step in range(STEPS + LAG):
            if step < STEPS:
                load_for(step + AHEAD)
                mixed[step] = mix_and_transpose(step)
            if 1 <= step <= STEPS:
                quantise_ctx(step - 1, mixed[step - 1])
            if step >= LAG:
                project(step - LAG)
